import numpy as np
import ml_dtypes


def mxq(x, axis, fmt="e4m3"):
    dtype, down = {"e4m3": (ml_dtypes.float8_e4m3fn, 7), "e5m2": (ml_dtypes.float8_e5m2, 14)}[fmt]
    v = np.moveaxis(np.asarray(x, np.float32).astype(ml_dtypes.bfloat16).astype(np.float64), axis, -1)
    blocks = v.reshape(v.shape[:-1] + (-1, 32))
    amax = np.abs(blocks).max(-1, keepdims=True)
    byte = np.maximum(np.where(amax > 0, np.frexp(amax)[1] - 1 + 127, 0) - down, 1)
    scale = np.exp2(byte - 127.0)
    codes = (blocks / scale).astype(np.float32).astype(dtype).astype(np.float64)
    return np.moveaxis((codes * scale).reshape(v.shape), -1, axis)


WIDE = False


def mx_kscale(k):
    if not WIDE:
        return np.ones(k)
    levels = np.array([10, -10, 5, -5, 0])
    a = np.random.permutation(np.resize(levels, k // 512 * 4)).reshape(k // 512, 4)
    idx = np.arange(k)
    return np.exp2(a[idx // 512, idx % 128 // 32])


BF16 = ml_dtypes.bfloat16


def bf(x):
    return np.asarray(x, np.float32).astype(BF16)


def f64(x):
    return np.asarray(x).astype(np.float64)


B, S, NI, NO = 16, 576, 256, 128


def setup_inputs():
    sn = mx_kscale(4 * NI)[::4]
    sc = NI ** -0.5

    def u():
        return bf(np.random.uniform(-sc, sc, (NO, NI)) / sn[None, :])

    return {"q_in": bf(np.random.standard_normal((B, S, 4 * NI)) * np.repeat(sn, 4)),
            "r_weight": u(), "i_weight": u(), "j_weight": u(), "k_weight": u()}


def reference(q_in, r_weight, i_weight, j_weight, k_weight):
    q = f64(q_in)
    V = np.stack([f64(r_weight), f64(i_weight), f64(j_weight), f64(k_weight)]).transpose(2, 0, 1).reshape(4 * NI, NO)
    Vq = mxq(V, 0, "e4m3")
    Wr, Wi, Wj, Wk = Vq.reshape(NI, 4, NO).transpose(1, 2, 0)
    W4 = np.stack([
        np.stack([Wr, -Wi, -Wj, -Wk]),
        np.stack([Wi, Wr, Wk, -Wj]),
        np.stack([Wj, -Wk, Wr, Wi]),
        np.stack([Wk, Wj, -Wi, Wr]),
    ])
    W = W4.transpose(3, 1, 2, 0).reshape(4 * NI, 4 * NO)
    return mxq(q, 2, "e4m3") @ W

@@ -1,0 +1,197 @@
+from contextlib import ExitStack
+
+import concourse.mybir as mybir
+from concourse.masks import make_identity
+
+BF16 = mybir.dt.bfloat16
+F32 = mybir.dt.float32
+U32 = mybir.dt.uint32
+U8 = mybir.dt.uint8
+FP8X4 = mybir.dt.float8_e4m3fn_x4
+
+P = 128
+TOKENS = 16 * 576
+K = 1024
+N_OUT = 512
+N_IN_Q = 256
+SLOTS = TOKENS // P
+FLOPS = 2 * TOKENS * K * N_OUT
+
+ROUNDS = [2, 2] + [4] * 17
+LOAD = 4
+X_BUFS = 12
+O_BUFS = 6
+MAXR = 4
+
+
+def tile_quaternionlinear_t_kernel(tc, q_in, r_weight, i_weight, j_weight, k_weight, out):
+    nc = tc.nc
+    assert sum(ROUNDS) == SLOTS
+    xin = q_in.flatten_outer_dims().rearrange("(p t) k -> p t k", t=SLOTS)
+    oview = out.flatten_outer_dims().rearrange("(p t) c -> p t c", t=SLOTS)
+
+    with ExitStack() as ctx:
+        const = ctx.enter_context(tc.tile_pool(name="const", bufs=1))
+        xpool = ctx.enter_context(tc.tile_pool(name="xpool", bufs=X_BUFS))
+        gpool = ctx.enter_context(tc.tile_pool(name="gpool", bufs=2))
+        cpool = ctx.enter_context(tc.tile_pool(name="cpool", bufs=3))
+        opool = ctx.enter_context(tc.tile_pool(name="opool", bufs=O_BUFS))
+        psum = ctx.enter_context(tc.psum_pool(name="psum", bufs=1))
+        ctx.enter_context(tc.manual_schedule())
+
+        ident = const.tile([P, P], F32, name="ident")
+        planes = const.tile([P, 9, N_IN_Q], BF16, name="planes")
+        wt = const.tile([P, 4, K], BF16, name="wt")
+        wgrp = const.tile([P, 2, 4 * N_OUT], BF16, name="wgrp", align_bytes=64)
+        wcodes = const.tile([P, 2, N_OUT], U32, name="wcodes", align_bytes=64)
+        wscl = const.tile([P, 2, N_OUT], U8, name="wscl", align_bytes=64)
+
+        for pos, w in ((0, i_weight), (1, r_weight), (2, k_weight), (5, j_weight), (7, r_weight), (8, i_weight)):
+            nc.sync.dma_start(out=planes[:, pos, :], in_=w)
+
+        n_chunks = SLOTS // LOAD
+        xt = {}
+
+        def load(c):
+            x_sb = xpool.tile([P, LOAD, K], BF16, name="x_sb", tag="x")
+            xt[c] = x_sb
+            if c == 0:
+                h = LOAD // 2
+                nc.sync.dma_start(out=x_sb[:, 0:h, :], in_=xin[:, 0:h, :])
+                nc.sync.dma_start(out=x_sb[:, h:LOAD, :], in_=xin[:, h:LOAD, :])
+            else:
+                nc.sync.dma_start(out=x_sb[:], in_=xin[:, c * LOAD:(c + 1) * LOAD, :])
+
+        for c in range(min(X_BUFS, n_chunks)):
+            load(c)
+
+        make_identity(nc, ident[:])
+
+        nc.vector.tensor_scalar_mul(out=planes[:, 3, :], in0=planes[:, 5, :], scalar1=-1.0)
+        nc.vector.tensor_scalar_mul(out=planes[:, 4, :], in0=planes[:, 0, :], scalar1=-1.0)
+        nc.vector.tensor_scalar_mul(out=planes[:, 6, :], in0=planes[:, 2, :], scalar1=-1.0)
+
+        def four(b):
+            return planes[:, b:b + 4, :].rearrange("p (a e) n -> p n a e", a=2)
+
+        def six(b):
+            v = planes[:, b:b + 6, :].rearrange("p (e x) n -> p e x n", e=2)
+            return v[:, :, 0:3:2, :].rearrange("p e a n -> p n a e")
+
+        def wt_view(d):
+            return wt[:, d, :].rearrange("p (n a e) -> p n a e", a=2, e=2)
+
+        nc.vector.tensor_copy(out=wt_view(1), in_=four(0))
+        nc.scalar.copy(out=wt_view(2), in_=four(5))
+        nc.vector.tensor_copy(out=wt_view(0), in_=six(1))
+        nc.vector.tensor_copy(out=wt_view(3), in_=six(2))
+
+        wgw = wgrp[:].bitcast(F32).rearrange("p g (m d x) -> p g m d x", d=2, x=4)
+        for d1 in range(2):
+            banks = []
+            for g in range(2):
+                wb = psum.tile([P, 4, P], F32, name="wb", tag="op%d" % (2 * d1 + g))
+                banks.append(wb)
+                for d0 in range(2):
+                    for u in range(2):
+                        s = 2 * g + u
+                        nc.tensor.transpose(
+                            out=wb[:, 2 * d0 + u, :],
+                            in_=wt[:, 2 * d1 + d0, :].bitcast(F32)[:, s * P:(s + 1) * P],
+                            identity=ident[:],
+                        )
+            nc.vector.tensor_copy(out=wgw[:, 0, :, d1, :], in_=banks[0][:].rearrange("p x m -> p m x"))
+            nc.scalar.copy(out=wgw[:, 1, :, d1, :], in_=banks[1][:].rearrange("p x m -> p m x"))
+        for g in range(2):
+            nc.vector.quantize_mx(out=wcodes[:, g, :].bitcast(FP8X4), scales=wscl[:, g, :], in_=wgrp[:, g, :])
+
+        starts = [sum(ROUNDS[:r]) for r in range(len(ROUNDS))]
+        n_rounds = len(ROUNDS)
+        tps = {}
+        grps = {}
+        cods = {}
+        next_load = [min(X_BUFS, n_chunks)]
+
+        def transposes(r):
+            for j in range(ROUNDS[r]):
+                t = starts[r] + j
+                c, l = divmod(t, LOAD)
+                tp = psum.tile([P, 4, P], F32, name="tp", tag="tp%d" % j)
+                tps[(r, j)] = tp
+                xw = xt[c][:, l, :].bitcast(F32)
+                for s in range(4):
+                    nc.tensor.transpose(out=tp[:, s, :], in_=xw[:, s * P:(s + 1) * P], identity=ident[:])
+                if l == LOAD - 1 and next_load[0] < n_chunks:
+                    load(next_load[0])
+                    next_load[0] += 1
+
+        def copies(r):
+            n = ROUNDS[r]
+            grp = gpool.tile([P, MAXR * K], BF16, name="grp", tag="grp", align_bytes=64)
+            grps[r] = grp
+            gw = grp[:].bitcast(F32).rearrange("p (j g k u) -> p j g k u", j=MAXR, g=2, u=2)
+            for j in range(n):
+                src = tps[(r, j)][:].rearrange("p (g u) k -> p g k u", g=2)
+                if j < (n + 1) // 2:
+                    nc.vector.tensor_copy(out=gw[:, j, :, :, :], in_=src)
+                else:
+                    nc.scalar.copy(out=gw[:, j, :, :, :], in_=src)
+
+        def quantise(r):
+            n = ROUNDS[r]
+            codes = cpool.tile([P, MAXR * 256], U32, name="codes", tag="codes", align_bytes=64)
+            scl = cpool.tile([P, MAXR * 256], U8, name="scl", tag="scl", align_bytes=64)
+            cods[r] = (codes, scl)
+            nc.vector.quantize_mx(
+                out=codes[:, 0:n * 256].bitcast(FP8X4),
+                scales=scl[:, 0:n * 256],
+                in_=grps[r][:, 0:n * K],
+            )
+
+        def multiply(r):
+            n = ROUNDS[r]
+            codes, scl = cods[r]
+            osb = opool.tile([P, MAXR, N_OUT], F32, name="osb", tag="osb")
+            for j in range(n):
+                acc = psum.tile([P, N_OUT], F32, name="acc", tag="op%d" % j)
+                for g in range(2):
+                    o = (2 * j + g) * P
+                    nc.tensor.matmul_mx(
+                        out=acc[:],
+                        lhsT=codes[:, o:o + P].bitcast(FP8X4),
+                        lhsT_scale=scl[:, o:o + P],
+                        rhs=wcodes[:, g, :].bitcast(FP8X4),
+                        rhs_scale=wscl[:, g, :],
+                        start=(g == 0),
+                        stop=(g == 1),
+                    )
+                tps[("o", r, j)] = acc
+            return osb
+
+        def drain(r, osb):
+            n = ROUNDS[r]
+            t0 = starts[r]
+            last = r == n_rounds - 1
+            for j in range(n):
+                acc = tps[("o", r, j)]
+                if j == 1:
+                    nc.vector.tensor_copy(out=osb[:, j, :], in_=acc[:])
+                else:
+                    nc.scalar.copy(out=osb[:, j, :], in_=acc[:])
+                if last and j >= 1:
+                    lo = 0 if j == 1 else j
+                    nc.scalar.dma_start(out=oview[:, t0 + lo:t0 + j + 1, :], in_=osb[:, lo:j + 1, :])
+            if not last:
+                nc.scalar.dma_start(out=oview[:, t0:t0 + n, :], in_=osb[:, 0:n, :])
+
+        transposes(0)
+        copies(0)
+        quantise(0)
+        for r in range(n_rounds):
+            if r + 1 < n_rounds:
+                transposes(r + 1)
+                copies(r + 1)
+            osb = multiply(r)
+            if r + 1 < n_rounds:
+                quantise(r + 1)
+            drain(r, osb)

@@ -19,8 +19,8 @@ FLOPS = 2 * TOKENS * K * N_OUT
 
 ROUNDS = [2, 2] + [4] * 17
 LOAD = 4
-X_BUFS = 12
-O_BUFS = 6
+X_BUFS = 9
+O_BUFS = 8
 MAXR = 4
 
 
@@ -180,9 +180,9 @@ def tile_quaternionlinear_t_kernel(tc, q_in, r_weight, i_weight, j_weight, k_wei
                     nc.scalar.copy(out=osb[:, j, :], in_=acc[:])
                 if last and j >= 1:
                     lo = 0 if j == 1 else j
-                    nc.scalar.dma_start(out=oview[:, t0 + lo:t0 + j + 1, :], in_=osb[:, lo:j + 1, :])
+                    nc.sync.dma_start(out=oview[:, t0 + lo:t0 + j + 1, :], in_=osb[:, lo:j + 1, :])
             if not last:
-                nc.scalar.dma_start(out=oview[:, t0:t0 + n, :], in_=osb[:, 0:n, :])
+                nc.sync.dma_start(out=oview[:, t0:t0 + n, :], in_=osb[:, 0:n, :])
 
         transposes(0)
         copies(0)

@@ -18,10 +18,13 @@ SLOTS = TOKENS // P
 FLOPS = 2 * TOKENS * K * N_OUT
 
 ROUNDS = [2, 2] + [4] * 17
-LOAD = 4
-X_BUFS = 9
-O_BUFS = 8
+LOAD = 8
+X_BUFS = 6
+O_BUFS = 4
 MAXR = 4
+FIRST_LOADS = [2, 2, 4]
+STORES = [4, 4] + [8] * 7 + [4, 2, 1, 1]
+MAXS = 8
 
 
 def tile_quaternionlinear_t_kernel(tc, q_in, r_weight, i_weight, j_weight, k_weight, out):
@@ -56,9 +59,10 @@ def tile_quaternionlinear_t_kernel(tc, q_in, r_weight, i_weight, j_weight, k_wei
             x_sb = xpool.tile([P, LOAD, K], BF16, name="x_sb", tag="x")
             xt[c] = x_sb
             if c == 0:
-                h = LOAD // 2
-                nc.sync.dma_start(out=x_sb[:, 0:h, :], in_=xin[:, 0:h, :])
-                nc.sync.dma_start(out=x_sb[:, h:LOAD, :], in_=xin[:, h:LOAD, :])
+                lo = 0
+                for n in FIRST_LOADS:
+                    nc.sync.dma_start(out=x_sb[:, lo:lo + n, :], in_=xin[:, lo:lo + n, :])
+                    lo += n
             else:
                 nc.sync.dma_start(out=x_sb[:], in_=xin[:, c * LOAD:(c + 1) * LOAD, :])
 
@@ -151,7 +155,6 @@ def tile_quaternionlinear_t_kernel(tc, q_in, r_weight, i_weight, j_weight, k_wei
         def multiply(r):
             n = ROUNDS[r]
             codes, scl = cods[r]
-            osb = opool.tile([P, MAXR, N_OUT], F32, name="osb", tag="osb")
             for j in range(n):
                 acc = psum.tile([P, N_OUT], F32, name="acc", tag="op%d" % j)
                 for g in range(2):
@@ -166,23 +169,31 @@ def tile_quaternionlinear_t_kernel(tc, q_in, r_weight, i_weight, j_weight, k_wei
                         stop=(g == 1),
                     )
                 tps[("o", r, j)] = acc
-            return osb
 
-        def drain(r, osb):
-            n = ROUNDS[r]
-            t0 = starts[r]
-            last = r == n_rounds - 1
-            for j in range(n):
+        group_of = {}
+        lo = 0
+        for n in STORES:
+            for t in range(lo, lo + n):
+                group_of[t] = (lo, n)
+            lo += n
+        assert lo == SLOTS
+        cur = {}
+
+        def drain(r):
+            for j in range(ROUNDS[r]):
+                t = starts[r] + j
+                g0, gn = group_of[t]
+                if t % MAXS == 0:
+                    cur["osb"] = opool.tile([P, MAXS, N_OUT], F32, name="osb", tag="osb")
+                osb = cur["osb"]
+                b = t % MAXS
                 acc = tps[("o", r, j)]
                 if j == 1:
-                    nc.vector.tensor_copy(out=osb[:, j, :], in_=acc[:])
+                    nc.vector.tensor_copy(out=osb[:, b, :], in_=acc[:])
                 else:
-                    nc.scalar.copy(out=osb[:, j, :], in_=acc[:])
-                if last and j >= 1:
-                    lo = 0 if j == 1 else j
-                    nc.sync.dma_start(out=oview[:, t0 + lo:t0 + j + 1, :], in_=osb[:, lo:j + 1, :])
-            if not last:
-                nc.sync.dma_start(out=oview[:, t0:t0 + n, :], in_=osb[:, 0:n, :])
+                    nc.scalar.copy(out=osb[:, b, :], in_=acc[:])
+                if t == g0 + gn - 1:
+                    nc.sync.dma_start(out=oview[:, g0:g0 + gn, :], in_=osb[:, b + 1 - gn:b + 1, :])
 
         transposes(0)
         copies(0)
@@ -191,7 +202,7 @@ def tile_quaternionlinear_t_kernel(tc, q_in, r_weight, i_weight, j_weight, k_wei
             if r + 1 < n_rounds:
                 transposes(r + 1)
                 copies(r + 1)
-            osb = multiply(r)
+            multiply(r)
             if r + 1 < n_rounds:
                 quantise(r + 1)
-            drain(r, osb)
+            drain(r)

@@ -193,7 +193,7 @@ def tile_quaternionlinear_t_kernel(tc, q_in, r_weight, i_weight, j_weight, k_wei
                 else:
                     nc.scalar.copy(out=osb[:, b, :], in_=acc[:])
                 if t == g0 + gn - 1:
-                    nc.sync.dma_start(out=oview[:, g0:g0 + gn, :], in_=osb[:, b + 1 - gn:b + 1, :])
+                    nc.scalar.dma_start(out=oview[:, g0:g0 + gn, :], in_=osb[:, b + 1 - gn:b + 1, :])
 
         transposes(0)
         copies(0)

@@ -23,7 +23,7 @@ X_BUFS = 6
 O_BUFS = 4
 MAXR = 4
 FIRST_LOADS = [2, 2, 4]
-STORES = [4, 4] + [8] * 7 + [4, 2, 1, 1]
+STORES = [4, 4] + [8] * 6 + [4, 4] + [2, 2, 2, 1, 1]
 MAXS = 8
 
 
@@ -43,13 +43,13 @@ def tile_quaternionlinear_t_kernel(tc, q_in, r_weight, i_weight, j_weight, k_wei
         ctx.enter_context(tc.manual_schedule())
 
         ident = const.tile([P, P], F32, name="ident")
-        planes = const.tile([P, 9, N_IN_Q], BF16, name="planes")
+        planes = const.tile([P, 11, N_IN_Q], BF16, name="planes")
         wt = const.tile([P, 4, K], BF16, name="wt")
         wgrp = const.tile([P, 2, 4 * N_OUT], BF16, name="wgrp", align_bytes=64)
         wcodes = const.tile([P, 2, N_OUT], U32, name="wcodes", align_bytes=64)
         wscl = const.tile([P, 2, N_OUT], U8, name="wscl", align_bytes=64)
 
-        for pos, w in ((0, i_weight), (1, r_weight), (2, k_weight), (5, j_weight), (7, r_weight), (8, i_weight)):
+        for pos, w in ((0, i_weight), (3, j_weight), (1, k_weight), (4, r_weight)):
             nc.sync.dma_start(out=planes[:, pos, :], in_=w)
 
         n_chunks = SLOTS // LOAD
@@ -71,27 +71,28 @@ def tile_quaternionlinear_t_kernel(tc, q_in, r_weight, i_weight, j_weight, k_wei
 
         make_identity(nc, ident[:])
 
-        nc.vector.tensor_scalar_mul(out=planes[:, 3, :], in0=planes[:, 5, :], scalar1=-1.0)
-        nc.vector.tensor_scalar_mul(out=planes[:, 4, :], in0=planes[:, 0, :], scalar1=-1.0)
-        nc.vector.tensor_scalar_mul(out=planes[:, 6, :], in0=planes[:, 2, :], scalar1=-1.0)
+        nc.vector.tensor_scalar_mul(out=planes[:, 2:6:3, :], in0=planes[:, 0:4:3, :], scalar1=-1.0)
+        nc.vector.tensor_scalar_mul(out=planes[:, 6:8, :], in0=planes[:, 0:2, :], scalar1=-1.0)
+        nc.scalar.copy(out=planes[:, 8, :], in_=planes[:, 0, :])
 
-        def four(b):
-            return planes[:, b:b + 4, :].rearrange("p (a e) n -> p n a e", a=2)
+        def near(b):
+            return planes[:, b:b + 4, :].rearrange("p (e a) n -> p n a e", e=2)
 
-        def six(b):
-            v = planes[:, b:b + 6, :].rearrange("p (e x) n -> p e x n", e=2)
-            return v[:, :, 0:3:2, :].rearrange("p e a n -> p n a e")
+        def far(b):
+            v = planes[:, b:b + 8, :].rearrange("p (e x) n -> p e x n", e=2)
+            return v[:, :, 0:2, :].rearrange("p e a n -> p n a e")
 
         def wt_view(d):
             return wt[:, d, :].rearrange("p (n a e) -> p n a e", a=2, e=2)
 
-        nc.vector.tensor_copy(out=wt_view(1), in_=four(0))
-        nc.scalar.copy(out=wt_view(2), in_=four(5))
-        nc.vector.tensor_copy(out=wt_view(0), in_=six(1))
-        nc.vector.tensor_copy(out=wt_view(3), in_=six(2))
+        nc.vector.tensor_copy(out=wt_view(1), in_=far(0))
+        nc.scalar.copy(out=wt_view(2), in_=far(3))
+        nc.vector.tensor_copy(out=wt_view(0), in_=near(4))
+        nc.vector.tensor_copy(out=wt_view(3), in_=near(1))
 
         wgw = wgrp[:].bitcast(F32).rearrange("p g (m d x) -> p g m d x", d=2, x=4)
-        for d1 in range(2):
+
+        def weight_half(d1):
             banks = []
             for g in range(2):
                 wb = psum.tile([P, 4, P], F32, name="wb", tag="op%d" % (2 * d1 + g))
@@ -106,8 +107,6 @@ def tile_quaternionlinear_t_kernel(tc, q_in, r_weight, i_weight, j_weight, k_wei
                         )
             nc.vector.tensor_copy(out=wgw[:, 0, :, d1, :], in_=banks[0][:].rearrange("p x m -> p m x"))
             nc.scalar.copy(out=wgw[:, 1, :, d1, :], in_=banks[1][:].rearrange("p x m -> p m x"))
-        for g in range(2):
-            nc.vector.quantize_mx(out=wcodes[:, g, :].bitcast(FP8X4), scales=wscl[:, g, :], in_=wgrp[:, g, :])
 
         starts = [sum(ROUNDS[:r]) for r in range(len(ROUNDS))]
         n_rounds = len(ROUNDS)
@@ -136,7 +135,7 @@ def tile_quaternionlinear_t_kernel(tc, q_in, r_weight, i_weight, j_weight, k_wei
             gw = grp[:].bitcast(F32).rearrange("p (j g k u) -> p j g k u", j=MAXR, g=2, u=2)
             for j in range(n):
                 src = tps[(r, j)][:].rearrange("p (g u) k -> p g k u", g=2)
-                if j < (n + 1) // 2:
+                if r > 0 and j < (n + 1) // 2:
                     nc.vector.tensor_copy(out=gw[:, j, :, :, :], in_=src)
                 else:
                     nc.scalar.copy(out=gw[:, j, :, :, :], in_=src)
@@ -193,11 +192,15 @@ def tile_quaternionlinear_t_kernel(tc, q_in, r_weight, i_weight, j_weight, k_wei
                 else:
                     nc.scalar.copy(out=osb[:, b, :], in_=acc[:])
                 if t == g0 + gn - 1:
-                    nc.scalar.dma_start(out=oview[:, g0:g0 + gn, :], in_=osb[:, b + 1 - gn:b + 1, :])
+                    nc.sync.dma_start(out=oview[:, g0:g0 + gn, :], in_=osb[:, b + 1 - gn:b + 1, :])
 
         transposes(0)
         copies(0)
+        weight_half(0)
         quantise(0)
+        weight_half(1)
+        for g in range(2):
+            nc.vector.quantize_mx(out=wcodes[:, g, :].bitcast(FP8X4), scales=wscl[:, g, :], in_=wgrp[:, g, :])
         for r in range(n_rounds):
             if r + 1 < n_rounds:
                 transposes(r + 1)

@@ -25,6 +25,7 @@ MAXR = 4
 FIRST_LOADS = [2, 2, 4]
 STORES = [4, 4] + [8] * 6 + [4, 4] + [2, 2, 2, 1, 1]
 MAXS = 8
+WARM = [6, 1, 1, 1, 3]
 
 
 def tile_quaternionlinear_t_kernel(tc, q_in, r_weight, i_weight, j_weight, k_weight, out):
@@ -70,6 +71,16 @@ def tile_quaternionlinear_t_kernel(tc, q_in, r_weight, i_weight, j_weight, k_wei
             load(c)
 
         make_identity(nc, ident[:])
+
+        zero = const.tile([P, N_OUT], BF16, name="zero")
+        nc.vector.memset(zero[:], 0.0)
+        warm = psum.tile([P, N_OUT], F32, name="warm", tag="tp3")
+
+        def keep_warm(n):
+            for i in range(n):
+                nc.tensor.matmul(out=warm[:], lhsT=zero[:, 0:P], rhs=zero[:], start=True, stop=True)
+
+        keep_warm(WARM[0])
 
         nc.vector.tensor_scalar_mul(out=planes[:, 2:6:3, :], in0=planes[:, 0:4:3, :], scalar1=-1.0)
         nc.vector.tensor_scalar_mul(out=planes[:, 6:8, :], in0=planes[:, 0:2, :], scalar1=-1.0)
@@ -196,15 +207,20 @@ def tile_quaternionlinear_t_kernel(tc, q_in, r_weight, i_weight, j_weight, k_wei
 
         transposes(0)
         copies(0)
+        keep_warm(WARM[1])
         weight_half(0)
         quantise(0)
+        keep_warm(WARM[2])
         weight_half(1)
+        keep_warm(WARM[3])
         for g in range(2):
             nc.vector.quantize_mx(out=wcodes[:, g, :].bitcast(FP8X4), scales=wscl[:, g, :], in_=wgrp[:, g, :])
         for r in range(n_rounds):
             if r + 1 < n_rounds:
                 transposes(r + 1)
                 copies(r + 1)
+            if r == 0:
+                keep_warm(WARM[4])
             multiply(r)
             if r + 1 < n_rounds:
                 quantise(r + 1)

@@ -22,10 +22,9 @@ LOAD = 8
 X_BUFS = 6
 O_BUFS = 4
 MAXR = 4
-FIRST_LOADS = [2, 2, 4]
+FIRST_LOADS = [1, 1, 2, 4]
 STORES = [4, 4] + [8] * 6 + [4, 4] + [2, 2, 2, 1, 1]
 MAXS = 8
-WARM = [6, 1, 1, 1, 3]
 
 
 def tile_quaternionlinear_t_kernel(tc, q_in, r_weight, i_weight, j_weight, k_weight, out):
@@ -71,16 +70,6 @@ def tile_quaternionlinear_t_kernel(tc, q_in, r_weight, i_weight, j_weight, k_wei
             load(c)
 
         make_identity(nc, ident[:])
-
-        zero = const.tile([P, N_OUT], BF16, name="zero")
-        nc.vector.memset(zero[:], 0.0)
-        warm = psum.tile([P, N_OUT], F32, name="warm", tag="tp3")
-
-        def keep_warm(n):
-            for i in range(n):
-                nc.tensor.matmul(out=warm[:], lhsT=zero[:, 0:P], rhs=zero[:], start=True, stop=True)
-
-        keep_warm(WARM[0])
 
         nc.vector.tensor_scalar_mul(out=planes[:, 2:6:3, :], in0=planes[:, 0:4:3, :], scalar1=-1.0)
         nc.vector.tensor_scalar_mul(out=planes[:, 6:8, :], in0=planes[:, 0:2, :], scalar1=-1.0)
@@ -198,7 +187,7 @@ def tile_quaternionlinear_t_kernel(tc, q_in, r_weight, i_weight, j_weight, k_wei
                 osb = cur["osb"]
                 b = t % MAXS
                 acc = tps[("o", r, j)]
-                if j == 1:
+                if j == 2:
                     nc.vector.tensor_copy(out=osb[:, b, :], in_=acc[:])
                 else:
                     nc.scalar.copy(out=osb[:, b, :], in_=acc[:])
@@ -207,20 +196,15 @@ def tile_quaternionlinear_t_kernel(tc, q_in, r_weight, i_weight, j_weight, k_wei
 
         transposes(0)
         copies(0)
-        keep_warm(WARM[1])
         weight_half(0)
         quantise(0)
-        keep_warm(WARM[2])
         weight_half(1)
-        keep_warm(WARM[3])
         for g in range(2):
             nc.vector.quantize_mx(out=wcodes[:, g, :].bitcast(FP8X4), scales=wscl[:, g, :], in_=wgrp[:, g, :])
         for r in range(n_rounds):
             if r + 1 < n_rounds:
                 transposes(r + 1)
                 copies(r + 1)
-            if r == 0:
-                keep_warm(WARM[4])
             multiply(r)
             if r + 1 < n_rounds:
                 quantise(r + 1)

@@ -40,7 +40,6 @@ def tile_quaternionlinear_t_kernel(tc, q_in, r_weight, i_weight, j_weight, k_wei
         cpool = ctx.enter_context(tc.tile_pool(name="cpool", bufs=3))
         opool = ctx.enter_context(tc.tile_pool(name="opool", bufs=O_BUFS))
         psum = ctx.enter_context(tc.psum_pool(name="psum", bufs=1))
-        ctx.enter_context(tc.manual_schedule())
 
         ident = const.tile([P, P], F32, name="ident")
         planes = const.tile([P, 11, N_IN_Q], BF16, name="planes")

from contextlib import ExitStack

import concourse.mybir as mybir
from concourse.masks import make_identity

BF16 = mybir.dt.bfloat16
F32 = mybir.dt.float32
U32 = mybir.dt.uint32
U8 = mybir.dt.uint8
FP8X4 = mybir.dt.float8_e4m3fn_x4

P = 128
TOKENS = 16 * 576
K = 1024
N_OUT = 512
N_IN_Q = 256
SLOTS = TOKENS // P
FLOPS = 2 * TOKENS * K * N_OUT

ROUNDS = [2, 2] + [4] * 17
LOAD = 8
X_BUFS = 6
O_BUFS = 4
MAXR = 4
FIRST_LOADS = [1, 1, 2, 4]
STORES = [4, 4] + [8] * 6 + [4, 4] + [2, 2, 2, 1, 1]
MAXS = 8


def tile_quaternionlinear_t_kernel(tc, q_in, r_weight, i_weight, j_weight, k_weight, out):
    nc = tc.nc
    assert sum(ROUNDS) == SLOTS
    xin = q_in.flatten_outer_dims().rearrange("(p t) k -> p t k", t=SLOTS)
    oview = out.flatten_outer_dims().rearrange("(p t) c -> p t c", t=SLOTS)

    with ExitStack() as ctx:
        const = ctx.enter_context(tc.tile_pool(name="const", bufs=1))
        xpool = ctx.enter_context(tc.tile_pool(name="xpool", bufs=X_BUFS))
        gpool = ctx.enter_context(tc.tile_pool(name="gpool", bufs=2))
        cpool = ctx.enter_context(tc.tile_pool(name="cpool", bufs=3))
        opool = ctx.enter_context(tc.tile_pool(name="opool", bufs=O_BUFS))
        psum = ctx.enter_context(tc.psum_pool(name="psum", bufs=1))

        ident = const.tile([P, P], F32, name="ident")
        planes = const.tile([P, 11, N_IN_Q], BF16, name="planes")
        wt = const.tile([P, 4, K], BF16, name="wt")
        wgrp = const.tile([P, 2, 4 * N_OUT], BF16, name="wgrp", align_bytes=64)
        wcodes = const.tile([P, 2, N_OUT], U32, name="wcodes", align_bytes=64)
        wscl = const.tile([P, 2, N_OUT], U8, name="wscl", align_bytes=64)

        for pos, w in ((0, i_weight), (3, j_weight), (1, k_weight), (4, r_weight)):
            nc.sync.dma_start(out=planes[:, pos, :], in_=w)

        n_chunks = SLOTS // LOAD
        xt = {}

        def load(c):
            x_sb = xpool.tile([P, LOAD, K], BF16, name="x_sb", tag="x")
            xt[c] = x_sb
            if c == 0:
                lo = 0
                for n in FIRST_LOADS:
                    nc.sync.dma_start(out=x_sb[:, lo:lo + n, :], in_=xin[:, lo:lo + n, :])
                    lo += n
            else:
                nc.sync.dma_start(out=x_sb[:], in_=xin[:, c * LOAD:(c + 1) * LOAD, :])

        for c in range(min(X_BUFS, n_chunks)):
            load(c)

        make_identity(nc, ident[:])

        nc.vector.tensor_scalar_mul(out=planes[:, 2:6:3, :], in0=planes[:, 0:4:3, :], scalar1=-1.0)
        nc.vector.tensor_scalar_mul(out=planes[:, 6:8, :], in0=planes[:, 0:2, :], scalar1=-1.0)
        nc.scalar.copy(out=planes[:, 8, :], in_=planes[:, 0, :])

        def near(b):
            return planes[:, b:b + 4, :].rearrange("p (e a) n -> p n a e", e=2)

        def far(b):
            v = planes[:, b:b + 8, :].rearrange("p (e x) n -> p e x n", e=2)
            return v[:, :, 0:2, :].rearrange("p e a n -> p n a e")

        def wt_view(d):
            return wt[:, d, :].rearrange("p (n a e) -> p n a e", a=2, e=2)

        nc.vector.tensor_copy(out=wt_view(1), in_=far(0))
        nc.scalar.copy(out=wt_view(2), in_=far(3))
        nc.vector.tensor_copy(out=wt_view(0), in_=near(4))
        nc.vector.tensor_copy(out=wt_view(3), in_=near(1))

        wgw = wgrp[:].bitcast(F32).rearrange("p g (m d x) -> p g m d x", d=2, x=4)

        def weight_half(d1):
            banks = []
            for g in range(2):
                wb = psum.tile([P, 4, P], F32, name="wb", tag="op%d" % (2 * d1 + g))
                banks.append(wb)
                for d0 in range(2):
                    for u in range(2):
                        s = 2 * g + u
                        nc.tensor.transpose(
                            out=wb[:, 2 * d0 + u, :],
                            in_=wt[:, 2 * d1 + d0, :].bitcast(F32)[:, s * P:(s + 1) * P],
                            identity=ident[:],
                        )
            nc.vector.tensor_copy(out=wgw[:, 0, :, d1, :], in_=banks[0][:].rearrange("p x m -> p m x"))
            nc.scalar.copy(out=wgw[:, 1, :, d1, :], in_=banks[1][:].rearrange("p x m -> p m x"))

        starts = [sum(ROUNDS[:r]) for r in range(len(ROUNDS))]
        n_rounds = len(ROUNDS)
        tps = {}
        grps = {}
        cods = {}
        next_load = [min(X_BUFS, n_chunks)]

        def transposes(r):
            for j in range(ROUNDS[r]):
                t = starts[r] + j
                c, l = divmod(t, LOAD)
                tp = psum.tile([P, 4, P], F32, name="tp", tag="tp%d" % j)
                tps[(r, j)] = tp
                xw = xt[c][:, l, :].bitcast(F32)
                for s in range(4):
                    nc.tensor.transpose(out=tp[:, s, :], in_=xw[:, s * P:(s + 1) * P], identity=ident[:])
                if l == LOAD - 1 and next_load[0] < n_chunks:
                    load(next_load[0])
                    next_load[0] += 1

        def copies(r):
            n = ROUNDS[r]
            grp = gpool.tile([P, MAXR * K], BF16, name="grp", tag="grp", align_bytes=64)
            grps[r] = grp
            gw = grp[:].bitcast(F32).rearrange("p (j g k u) -> p j g k u", j=MAXR, g=2, u=2)
            for j in range(n):
                src = tps[(r, j)][:].rearrange("p (g u) k -> p g k u", g=2)
                if r > 0 and j < (n + 1) // 2:
                    nc.vector.tensor_copy(out=gw[:, j, :, :, :], in_=src)
                else:
                    nc.scalar.copy(out=gw[:, j, :, :, :], in_=src)

        def quantise(r):
            n = ROUNDS[r]
            codes = cpool.tile([P, MAXR * 256], U32, name="codes", tag="codes", align_bytes=64)
            scl = cpool.tile([P, MAXR * 256], U8, name="scl", tag="scl", align_bytes=64)
            cods[r] = (codes, scl)
            nc.vector.quantize_mx(
                out=codes[:, 0:n * 256].bitcast(FP8X4),
                scales=scl[:, 0:n * 256],
                in_=grps[r][:, 0:n * K],
            )

        def multiply(r):
            n = ROUNDS[r]
            codes, scl = cods[r]
            for j in range(n):
                acc = psum.tile([P, N_OUT], F32, name="acc", tag="op%d" % j)
                for g in range(2):
                    o = (2 * j + g) * P
                    nc.tensor.matmul_mx(
                        out=acc[:],
                        lhsT=codes[:, o:o + P].bitcast(FP8X4),
                        lhsT_scale=scl[:, o:o + P],
                        rhs=wcodes[:, g, :].bitcast(FP8X4),
                        rhs_scale=wscl[:, g, :],
                        start=(g == 0),
                        stop=(g == 1),
                    )
                tps[("o", r, j)] = acc

        group_of = {}
        lo = 0
        for n in STORES:
            for t in range(lo, lo + n):
                group_of[t] = (lo, n)
            lo += n
        assert lo == SLOTS
        cur = {}

        def drain(r):
            for j in range(ROUNDS[r]):
                t = starts[r] + j
                g0, gn = group_of[t]
                if t % MAXS == 0:
                    cur["osb"] = opool.tile([P, MAXS, N_OUT], F32, name="osb", tag="osb")
                osb = cur["osb"]
                b = t % MAXS
                acc = tps[("o", r, j)]
                if j == 2:
                    nc.vector.tensor_copy(out=osb[:, b, :], in_=acc[:])
                else:
                    nc.scalar.copy(out=osb[:, b, :], in_=acc[:])
                if t == g0 + gn - 1:
                    nc.sync.dma_start(out=oview[:, g0:g0 + gn, :], in_=osb[:, b + 1 - gn:b + 1, :])

        transposes(0)
        copies(0)
        weight_half(0)
        quantise(0)
        weight_half(1)
        for g in range(2):
            nc.vector.quantize_mx(out=wcodes[:, g, :].bitcast(FP8X4), scales=wscl[:, g, :], in_=wgrp[:, g, :])
        for r in range(n_rounds):
            if r + 1 < n_rounds:
                transposes(r + 1)
                copies(r + 1)
            multiply(r)
            if r + 1 < n_rounds:
                quantise(r + 1)
            drain(r)
